import numpy as np
import ml_dtypes


def mxq(x, axis, fmt="e4m3"):
    dtype, down = {"e4m3": (ml_dtypes.float8_e4m3fn, 7), "e5m2": (ml_dtypes.float8_e5m2, 14)}[fmt]
    v = np.moveaxis(np.asarray(x, np.float32).astype(ml_dtypes.bfloat16).astype(np.float64), axis, -1)
    blocks = v.reshape(v.shape[:-1] + (-1, 32))
    amax = np.abs(blocks).max(-1, keepdims=True)
    byte = np.maximum(np.where(amax > 0, np.frexp(amax)[1] - 1 + 127, 0) - down, 1)
    scale = np.exp2(byte - 127.0)
    codes = (blocks / scale).astype(np.float32).astype(dtype).astype(np.float64)
    return np.moveaxis((codes * scale).reshape(v.shape), -1, axis)


WIDE = False


def mx_kscale(k):
    if not WIDE:
        return np.ones(k)
    levels = np.array([10, -10, 5, -5, 0])
    a = np.random.permutation(np.resize(levels, k // 512 * 4)).reshape(k // 512, 4)
    idx = np.arange(k)
    return np.exp2(a[idx // 512, idx % 128 // 32])


BF16 = ml_dtypes.bfloat16


def bf(x):
    return np.asarray(x, np.float32).astype(BF16)


def f64(x):
    return np.asarray(x).astype(np.float64)


E2M1 = np.array([0.0, 0.5, 1.0, 1.5, 2.0, 3.0, 4.0, 6.0, -0.0, -0.5, -1.0, -1.5, -2.0, -3.0, -4.0, -6.0])


def pack_weight(w, fmt):
    k, n = w.shape
    w = f64(bf(w)).reshape(k // 32, 32, n)
    amax = np.abs(w).max(1)
    if fmt == "e4m3":
        byte = np.frexp(amax)[1] - 1 + 127 - 7
    else:
        mant, ex = np.frexp(amax / 6.0)
        byte = np.where(mant > 0.5, ex, ex - 1) + 127
    byte = np.clip(np.where(amax > 0, byte, 1), 1, 254)
    scaled = (w * np.exp2(127.0 - byte)[:, None, :]).reshape(k, n).astype(np.float32)
    by_word = np.ascontiguousarray(scaled.reshape(k // 512, 128, 4, n).transpose(0, 1, 3, 2))
    if fmt == "e4m3":
        words = by_word.astype(ml_dtypes.float8_e4m3fn).view(np.uint8)
    else:
        c = by_word.astype(ml_dtypes.float4_e2m1fn).view(np.uint8) & 0xF
        words = c[..., 0::2] | (c[..., 1::2] << 4)
    return np.ascontiguousarray(words), np.ascontiguousarray(byte.astype(np.uint8).reshape(k // 512, 16, n))


def unpack_weight(words, scales, fmt):
    g, p, n, _ = words.shape
    if fmt == "e4m3":
        vals = np.ascontiguousarray(words).view(ml_dtypes.float8_e4m3fn).astype(np.float64)
    else:
        nib = np.empty((g, p, n, 4), np.uint8)
        nib[..., 0::2] = words & 0xF
        nib[..., 1::2] = words >> 4
        vals = E2M1[nib]
    vals = vals * np.repeat(np.exp2(scales.astype(np.float64) - 127.0), 8, axis=1)[..., None]
    return vals.transpose(0, 1, 3, 2).reshape(g * 512, n)

def pack4(w):
    words, scales = pack_weight(w, "e2m1")
    return words.reshape(words.shape[0], 128, -1), scales


def unpack4(words, scales):
    return unpack_weight(words.reshape(words.shape[0], 128, -1, 2), scales, "e2m1")


B, S, HID, H, HK, D = 2, 64, 16384, 16, 4, 128
EPS = 1e-6
PRE = 0.004


def rmsnorm(v, w):
    var = np.mean(v * v, axis=-1, keepdims=True)
    return w * (v * (1.0 / np.sqrt(var + EPS)))


def rope(v, cos, sin):
    c = cos[:, :, None, :]
    sn = sin[:, :, None, :]
    v1, v2 = np.split(v, 2, axis=-1)
    rot = np.concatenate([-v2, v1], axis=-1)
    return v * c + rot * sn


def setup_inputs():
    s = mx_kscale(HID)
    hidden_states = bf(np.random.standard_normal((B, S, HID)) * s)
    cos = bf(np.cos(np.random.standard_normal((B, S, D))))
    sin = bf(np.sin(np.random.standard_normal((B, S, D))))
    wq = np.random.standard_normal((H * D, HID)) * PRE / np.sqrt(HID) / s
    wk = np.random.standard_normal((HK * D, HID)) * PRE / np.sqrt(HID) / s
    q_norm_w = bf(1.0 + 0.1 * np.random.standard_normal(D))
    k_norm_w = bf(1.0 + 0.1 * np.random.standard_normal(D))
    wq_words, wq_scales = pack4(np.ascontiguousarray(wq.T))
    wk_words, wk_scales = pack4(np.ascontiguousarray(wk.T))
    return {
        "hidden_states": hidden_states,
        "cos": cos,
        "sin": sin,
        "Wq_query_words": wq_words,
        "Wq_query_scales": wq_scales,
        "Wk_words": wk_words,
        "Wk_scales": wk_scales,
        "q_norm_w": q_norm_w,
        "k_norm_w": k_norm_w,
    }


def reference(hidden_states, cos, sin, Wq_query_words, Wq_query_scales, Wk_words, Wk_scales, q_norm_w, k_norm_w):
    xq = mxq(f64(hidden_states), 2, "e4m3")
    q = (xq @ unpack4(Wq_query_words, Wq_query_scales)).reshape(B, S, H, D)
    k = (xq @ unpack4(Wk_words, Wk_scales)).reshape(B, S, HK, D)
    q = rmsnorm(q, f64(q_norm_w))
    k = rmsnorm(k, f64(k_norm_w))
    q = rope(q, f64(cos), f64(sin))
    k = rope(k, f64(cos), f64(sin))
    return q, k

@@ -1,0 +1,271 @@
+from contextlib import ExitStack
+
+import concourse.masks as masks
+import concourse.mybir as mybir
+
+F32 = mybir.dt.float32
+BF16 = mybir.dt.bfloat16
+I32 = mybir.dt.int32
+U32 = mybir.dt.uint32
+U8 = mybir.dt.uint8
+FP8X4 = mybir.dt.float8_e4m3fn_x4
+FP4X4 = mybir.dt.float4_e2m1fn_x4
+ACT = mybir.ActivationFunctionType
+ALU = mybir.AluOpType
+
+P = 128
+TOKENS = 128
+HIDDEN = 16384
+PACK = 4
+K_PASS = P * PACK
+GROUPS = HIDDEN // K_PASS
+HEAD = 128
+HALF = HEAD // 2
+EPS = 1e-6
+
+BLOCK = 512
+BLOCK_HEADS = BLOCK // HEAD
+Q_BLOCKS = 4
+K_BLOCK = 4
+BLOCKS = 5
+WORD_BYTES = BLOCK * 2
+
+CHUNK = 4
+PERIOD = 8
+PERIODS = GROUPS // PERIOD
+PERIOD_CHUNKS = PERIOD // CHUNK
+
+X_LOAD = 8
+QUANT = 4
+BANK = 2
+
+FLOPS = 2 * TOKENS * HIDDEN * BLOCKS * BLOCK
+
+
+def tile_qwen3nextattentionforengine_pa_k_kernel(
+    tc,
+    hidden_states,
+    cos,
+    sin,
+    Wq_query_words,
+    Wq_query_scales,
+    Wk_words,
+    Wk_scales,
+    q_norm_w,
+    k_norm_w,
+    out_0,
+    out_1,
+):
+    nc = tc.nc
+    x_rows = hidden_states.rearrange("b s k -> (b s) k")
+    wq_words = Wq_query_words.bitcast(I32)
+    wk_words = Wk_words.bitcast(I32)
+    wq_scales = Wq_query_scales.bitcast(I32)
+    wk_scales = Wk_scales.bitcast(I32)
+    out_q = out_0.rearrange("b s h d -> (b s) (h d)")
+    out_k = out_1.rearrange("b s h d -> (b s) (h d)")
+
+    with ExitStack() as ctx:
+        ctx.enter_context(tc.manual_schedule())
+        keep = ctx.enter_context(tc.tile_pool(name="keep", bufs=1))
+        ring = ctx.enter_context(tc.tile_pool(name="ring", bufs=2 * PERIOD_CHUNKS))
+        sums = ctx.enter_context(tc.psum_pool(name="sums", bufs=1))
+
+        x_codes = keep.tile([P, GROUPS, TOKENS], U32, name="x_codes", align_bytes=64)
+        x_scales = keep.tile([P, GROUPS, TOKENS], U8, name="x_scales", align_bytes=64)
+        planes = [
+            keep.tile([P, PERIOD, BLOCKS * BLOCK], U8, name="planes%d" % s, align_bytes=64)
+            for s in range(2)
+        ]
+        acc = [sums.tile([P, BLOCK], F32, name="acc%d" % b) for b in range(BLOCKS)]
+        ident = keep.tile([P, P], F32, name="ident")
+        eps = keep.tile([P, 1], F32, name="eps")
+        warm = keep.tile([P, 1], F32, name="warm")
+        cos_sb = keep.tile([P, HEAD], BF16, name="cos_sb")
+        sin_sb = keep.tile([P, HEAD], BF16, name="sin_sb")
+        gain = [keep.tile([P, HEAD], BF16, name="gain%d" % i) for i in range(2)]
+        straight_tab = [keep.tile([P, HEAD], F32, name="straight_tab%d" % i) for i in range(2)]
+        crossed_tab = [keep.tile([P, HEAD], F32, name="crossed_tab%d" % i) for i in range(2)]
+
+        def load_scales(period):
+            g0 = period * PERIOD
+            plane = planes[period % 2]
+            for rows, first, width in ((wq_scales, 0, Q_BLOCKS * BLOCK), (wk_scales, K_BLOCK * BLOCK, BLOCK)):
+                for q in range(8):
+                    low = 32 * (q // 4) + q % 4
+                    nc.sync.dma_start(
+                        out=plane[low:P:64, :, first : first + width].bitcast(I32),
+                        in_=rows[g0 : g0 + PERIOD, q:16:8, :].rearrange("g q n -> q g n"),
+                    )
+
+        def load_words(chunk):
+            g0 = chunk * CHUNK
+            words = ring.tile([P, CHUNK, BLOCKS * WORD_BYTES], U8, name="words", align_bytes=64)
+            nc.sync.dma_start(
+                out=words[:, :, 0 : Q_BLOCKS * WORD_BYTES].bitcast(I32),
+                in_=wq_words[g0 : g0 + CHUNK].rearrange("g p b -> p g b"),
+            )
+            nc.sync.dma_start(
+                out=words[:, :, K_BLOCK * WORD_BYTES :].bitcast(I32),
+                in_=wk_words[g0 : g0 + CHUNK].rearrange("g p b -> p g b"),
+            )
+            return words
+
+        def project(g, block, words):
+            nc.tensor.matmul_mx(
+                out=acc[block][:],
+                lhsT=x_codes[:, g, :].bitcast(FP8X4),
+                lhsT_scale=x_scales[:, g, :],
+                rhs=words.bitcast(FP4X4),
+                rhs_scale=planes[(g // PERIOD) % 2][:, g % PERIOD, block * BLOCK : (block + 1) * BLOCK],
+                start=(g == 0),
+                stop=(g == GROUPS - 1),
+            )
+
+        nc.vector.memset(eps[:], EPS)
+        for plane in planes:
+            nc.vector.memset(plane[:].bitcast(I32), 0)
+        masks.make_identity(nc, ident[:])
+        nc.scalar.dma_start(out=cos_sb[:], in_=cos.rearrange("b s d -> (b s) d"))
+        nc.scalar.dma_start(out=sin_sb[:], in_=sin.rearrange("b s d -> (b s) d"))
+        nc.scalar.dma_start(out=gain[0][:], in_=q_norm_w.partition_broadcast(P))
+        nc.scalar.dma_start(out=gain[1][:], in_=k_norm_w.partition_broadcast(P))
+        nc.scalar.activation(out=warm[:], in_=eps[:], func=ACT.Sqrt)
+
+        with ExitStack() as head:
+            x_pool = head.enter_context(tc.tile_pool(name="x_pool", bufs=GROUPS // X_LOAD))
+            stage = head.enter_context(tc.tile_pool(name="stage", bufs=2))
+            flipped = head.enter_context(tc.psum_pool(name="flipped", bufs=3))
+
+            x_raw = []
+            for c in range(GROUPS // X_LOAD):
+                raw = x_pool.tile([P, X_LOAD * K_PASS], BF16, name="raw")
+                nc.sync.dma_start(out=raw[:], in_=x_rows[:, c * X_LOAD * K_PASS : (c + 1) * X_LOAD * K_PASS])
+                x_raw.append(raw)
+
+            for g0 in range(0, GROUPS, QUANT):
+                pairs = x_raw[g0 // X_LOAD][:].bitcast(F32)
+                grouped = stage.tile([P, QUANT, TOKENS, PACK], BF16, name="grouped", align_bytes=64)
+                for b0 in range(0, QUANT, BANK):
+                    xt = flipped.tile([P, BANK, 2, TOKENS], F32, name="xt")
+                    for i in range(BANK):
+                        first = ((g0 + b0 + i) % X_LOAD) * (K_PASS // 2)
+                        for u in range(2):
+                            nc.tensor.transpose(
+                                xt[:, i, u, :], pairs[:, first + u : first + K_PASS // 2 : 2], ident[:]
+                            )
+                    nc.scalar.copy(
+                        out=grouped[:, b0 : b0 + BANK, :, :].bitcast(F32),
+                        in_=xt[:].rearrange("p g u m -> p g m u"),
+                    )
+                nc.vector.quantize_mx(
+                    out=x_codes[:, g0 : g0 + QUANT, :].rearrange("p g m -> p (g m)").bitcast(FP8X4),
+                    scales=x_scales[:, g0 : g0 + QUANT, :].rearrange("p g m -> p (g m)"),
+                    in_=grouped[:].rearrange("p g m t -> p (g m t)"),
+                )
+
+        words_of = {}
+        for period in range(2):
+            load_scales(period)
+            for chunk in range(period * PERIOD_CHUNKS, (period + 1) * PERIOD_CHUNKS):
+                words_of[chunk] = load_words(chunk)
+
+        for i in range(2):
+            nc.vector.tensor_tensor(out=straight_tab[i][:], in0=cos_sb[:], in1=gain[i][:], op=ALU.mult)
+            nc.vector.scalar_tensor_tensor(
+                out=crossed_tab[i][:, 0:HALF],
+                in0=sin_sb[:, 0:HALF],
+                scalar=-1.0,
+                in1=gain[i][:, HALF:HEAD],
+                op0=ALU.mult,
+                op1=ALU.mult,
+            )
+            nc.vector.tensor_tensor(
+                out=crossed_tab[i][:, HALF:HEAD], in0=sin_sb[:, HALF:HEAD], in1=gain[i][:, 0:HALF], op=ALU.mult
+            )
+
+        tail = ctx.enter_context(tc.tile_pool(name="tail", bufs=BLOCKS * PERIOD_CHUNKS))
+        work = ctx.enter_context(tc.tile_pool(name="work", bufs=2))
+
+        def finish(block):
+            i = 0 if block < Q_BLOCKS else 1
+            dest = out_q[:, block * BLOCK : (block + 1) * BLOCK] if block < Q_BLOCKS else out_k
+            heads = acc[block][:].rearrange("p (h d) -> p h d", d=HEAD)
+            v = work.tile([P, BLOCK_HEADS, HEAD], F32, name="v")
+            squares = work.tile([P, BLOCK_HEADS, HEAD], F32, name="squares")
+            sum_sq = work.tile([P, BLOCK_HEADS], F32, name="sum_sq")
+            rms = work.tile([P, BLOCK_HEADS], F32, name="rms")
+            inv_rms = work.tile([P, BLOCK_HEADS], F32, name="inv_rms")
+            straight = work.tile([P, BLOCK_HEADS, HEAD], F32, name="straight")
+            crossed = work.tile([P, BLOCK_HEADS, HEAD], F32, name="crossed")
+            result = work.tile([P, BLOCK_HEADS, HEAD], F32, name="result")
+
+            nc.scalar.copy(out=v[:], in_=heads)
+            for h in range(BLOCK_HEADS):
+                nc.scalar.activation(
+                    out=squares[:, h, :], in_=heads[:, h, :], func=ACT.Square, accum_out=sum_sq[:, h : h + 1]
+                )
+            nc.scalar.activation(out=rms[:], in_=sum_sq[:], func=ACT.Sqrt, scale=1.0 / HEAD, bias=eps[:])
+
+            nc.vector.tensor_tensor(
+                out=straight[:],
+                in0=v[:],
+                in1=straight_tab[i][:].unsqueeze(1).to_broadcast([P, BLOCK_HEADS, HEAD]),
+                op=ALU.mult,
+            )
+            nc.vector.tensor_tensor(
+                out=crossed[:, :, 0:HALF],
+                in0=v[:, :, HALF:HEAD],
+                in1=crossed_tab[i][:, 0:HALF].unsqueeze(1).to_broadcast([P, BLOCK_HEADS, HALF]),
+                op=ALU.mult,
+            )
+            nc.vector.tensor_tensor(
+                out=crossed[:, :, HALF:HEAD],
+                in0=v[:, :, 0:HALF],
+                in1=crossed_tab[i][:, HALF:HEAD].unsqueeze(1).to_broadcast([P, BLOCK_HEADS, HALF]),
+                op=ALU.mult,
+            )
+            nc.vector.tensor_tensor(out=straight[:], in0=straight[:], in1=crossed[:], op=ALU.add)
+            nc.vector.reciprocal(out=inv_rms[:], in_=rms[:])
+            nc.vector.tensor_tensor(
+                out=result[:],
+                in0=straight[:],
+                in1=inv_rms[:].unsqueeze(2).to_broadcast([P, BLOCK_HEADS, HEAD]),
+                op=ALU.mult,
+            )
+            nc.sync.dma_start(out=dest, in_=result[:].rearrange("p h d -> p (h d)"))
+
+        last_blocks = [K_BLOCK] + list(range(Q_BLOCKS))
+        last_words = {}
+        for period in range(PERIODS - 1):
+            for chunk in range(period * PERIOD_CHUNKS, (period + 1) * PERIOD_CHUNKS):
+                for i in range(CHUNK):
+                    for block in range(BLOCKS):
+                        project(
+                            chunk * CHUNK + i,
+                            block,
+                            words_of[chunk][:, i, block * WORD_BYTES : (block + 1) * WORD_BYTES],
+                        )
+            ahead = period + 2
+            if ahead < PERIODS - 1:
+                load_scales(ahead)
+                for chunk in range(ahead * PERIOD_CHUNKS, (ahead + 1) * PERIOD_CHUNKS):
+                    words_of[chunk] = load_words(chunk)
+            if ahead == PERIODS - 1:
+                load_scales(ahead)
+                for block in last_blocks:
+                    for chunk in range(ahead * PERIOD_CHUNKS, (ahead + 1) * PERIOD_CHUNKS):
+                        g0 = chunk * CHUNK
+                        piece = tail.tile([P, CHUNK, WORD_BYTES], U8, name="piece", align_bytes=64)
+                        if block < Q_BLOCKS:
+                            source = wq_words[g0 : g0 + CHUNK, :, block * (WORD_BYTES // 4) : (block + 1) * (WORD_BYTES // 4)]
+                        else:
+                            source = wk_words[g0 : g0 + CHUNK]
+                        nc.sync.dma_start(out=piece[:].bitcast(I32), in_=source.rearrange("g p b -> p g b"))
+                        last_words[(block, chunk)] = piece
+
+        for block in last_blocks:
+            for chunk in range((PERIODS - 1) * PERIOD_CHUNKS, PERIODS * PERIOD_CHUNKS):
+                for i in range(CHUNK):
+                    project(chunk * CHUNK + i, block, last_words[(block, chunk)][:, i, :])
+            finish(block)

@@ -60,8 +60,8 @@ def tile_qwen3nextattentionforengine_pa_k_kernel(
     x_rows = hidden_states.rearrange("b s k -> (b s) k")
     wq_words = Wq_query_words.bitcast(I32)
     wk_words = Wk_words.bitcast(I32)
-    wq_scales = Wq_query_scales.bitcast(I32)
-    wk_scales = Wk_scales.bitcast(I32)
+    wq_scales = Wq_query_scales.bitcast(F32)
+    wk_scales = Wk_scales.bitcast(F32)
     out_q = out_0.rearrange("b s h d -> (b s) (h d)")
     out_k = out_1.rearrange("b s h d -> (b s) (h d)")
 
@@ -93,8 +93,8 @@ def tile_qwen3nextattentionforengine_pa_k_kernel(
             for rows, first, width in ((wq_scales, 0, Q_BLOCKS * BLOCK), (wk_scales, K_BLOCK * BLOCK, BLOCK)):
                 for q in range(8):
                     low = 32 * (q // 4) + q % 4
-                    nc.sync.dma_start(
-                        out=plane[low:P:64, :, first : first + width].bitcast(I32),
+                    nc.gpsimd.dma_start(
+                        out=plane[low:P:64, :, first : first + width].bitcast(F32),
                         in_=rows[g0 : g0 + PERIOD, q:16:8, :].rearrange("g q n -> q g n"),
                     )
 
@@ -123,9 +123,9 @@ def tile_qwen3nextattentionforengine_pa_k_kernel(
             )
 
         nc.vector.memset(eps[:], EPS)
-        for plane in planes:
-            nc.vector.memset(plane[:].bitcast(I32), 0)
+        nc.vector.memset(planes[0][:].bitcast(I32), 0)
         masks.make_identity(nc, ident[:])
+        load_scales(0)
         nc.scalar.dma_start(out=cos_sb[:], in_=cos.rearrange("b s d -> (b s) d"))
         nc.scalar.dma_start(out=sin_sb[:], in_=sin.rearrange("b s d -> (b s) d"))
         nc.scalar.dma_start(out=gain[0][:], in_=q_norm_w.partition_broadcast(P))
@@ -164,9 +164,10 @@ def tile_qwen3nextattentionforengine_pa_k_kernel(
                     in_=grouped[:].rearrange("p g m t -> p (g m t)"),
                 )
 
+        nc.vector.memset(planes[1][:].bitcast(I32), 0)
+        load_scales(1)
         words_of = {}
         for period in range(2):
-            load_scales(period)
             for chunk in range(period * PERIOD_CHUNKS, (period + 1) * PERIOD_CHUNKS):
                 words_of[chunk] = load_words(chunk)
 

@@ -34,6 +34,7 @@ CHUNK = 4
 PERIOD = 8
 PERIODS = GROUPS // PERIOD
 PERIOD_CHUNKS = PERIOD // CHUNK
+RING = 3
 
 X_LOAD = 8
 QUANT = 4
@@ -68,14 +69,14 @@ def tile_qwen3nextattentionforengine_pa_k_kernel(
     with ExitStack() as ctx:
         ctx.enter_context(tc.manual_schedule())
         keep = ctx.enter_context(tc.tile_pool(name="keep", bufs=1))
-        ring = ctx.enter_context(tc.tile_pool(name="ring", bufs=2 * PERIOD_CHUNKS))
+        ring = ctx.enter_context(tc.tile_pool(name="ring", bufs=RING))
         sums = ctx.enter_context(tc.psum_pool(name="sums", bufs=1))
 
         x_codes = keep.tile([P, GROUPS, TOKENS], U32, name="x_codes", align_bytes=64)
         x_scales = keep.tile([P, GROUPS, TOKENS], U8, name="x_scales", align_bytes=64)
         planes = [
             keep.tile([P, PERIOD, BLOCKS * BLOCK], U8, name="planes%d" % s, align_bytes=64)
-            for s in range(2)
+            for s in range(PERIODS)
         ]
         acc = [sums.tile([P, BLOCK], F32, name="acc%d" % b) for b in range(BLOCKS)]
         ident = keep.tile([P, P], F32, name="ident")
@@ -89,13 +90,12 @@ def tile_qwen3nextattentionforengine_pa_k_kernel(
 
         def load_scales(period):
             g0 = period * PERIOD
-            plane = planes[period % 2]
+            plane = planes[period]
             for rows, first, width in ((wq_scales, 0, Q_BLOCKS * BLOCK), (wk_scales, K_BLOCK * BLOCK, BLOCK)):
-                for q in range(8):
-                    low = 32 * (q // 4) + q % 4
+                for r in range(4):
                     nc.gpsimd.dma_start(
-                        out=plane[low:P:64, :, first : first + width].bitcast(F32),
-                        in_=rows[g0 : g0 + PERIOD, q:16:8, :].rearrange("g q n -> q g n"),
+                        out=plane[r:P:32, :, first : first + width].bitcast(F32),
+                        in_=rows[g0 : g0 + PERIOD, r:16:4, :].rearrange("g q n -> q g n"),
                     )
 
         def load_words(chunk):
@@ -117,15 +117,17 @@ def tile_qwen3nextattentionforengine_pa_k_kernel(
                 lhsT=x_codes[:, g, :].bitcast(FP8X4),
                 lhsT_scale=x_scales[:, g, :],
                 rhs=words.bitcast(FP4X4),
-                rhs_scale=planes[(g // PERIOD) % 2][:, g % PERIOD, block * BLOCK : (block + 1) * BLOCK],
+                rhs_scale=planes[g // PERIOD][:, g % PERIOD, block * BLOCK : (block + 1) * BLOCK],
                 start=(g == 0),
                 stop=(g == GROUPS - 1),
             )
 
         nc.vector.memset(eps[:], EPS)
-        nc.vector.memset(planes[0][:].bitcast(I32), 0)
+        for plane in planes:
+            nc.vector.memset(plane[:].bitcast(I32), 0)
         masks.make_identity(nc, ident[:])
-        load_scales(0)
+        for period in range(PERIODS):
+            load_scales(period)
         nc.scalar.dma_start(out=cos_sb[:], in_=cos.rearrange("b s d -> (b s) d"))
         nc.scalar.dma_start(out=sin_sb[:], in_=sin.rearrange("b s d -> (b s) d"))
         nc.scalar.dma_start(out=gain[0][:], in_=q_norm_w.partition_broadcast(P))
@@ -164,12 +166,9 @@ def tile_qwen3nextattentionforengine_pa_k_kernel(
                     in_=grouped[:].rearrange("p g m t -> p (g m t)"),
                 )
 
-        nc.vector.memset(planes[1][:].bitcast(I32), 0)
-        load_scales(1)
         words_of = {}
-        for period in range(2):
-            for chunk in range(period * PERIOD_CHUNKS, (period + 1) * PERIOD_CHUNKS):
-                words_of[chunk] = load_words(chunk)
+        for chunk in range(RING):
+            words_of[chunk] = load_words(chunk)
 
         for i in range(2):
             nc.vector.tensor_tensor(out=straight_tab[i][:], in0=cos_sb[:], in1=gain[i][:], op=ALU.mult)
@@ -238,32 +237,29 @@ def tile_qwen3nextattentionforengine_pa_k_kernel(
 
         last_blocks = [K_BLOCK] + list(range(Q_BLOCKS))
         last_words = {}
-        for period in range(PERIODS - 1):
-            for chunk in range(period * PERIOD_CHUNKS, (period + 1) * PERIOD_CHUNKS):
-                for i in range(CHUNK):
-                    for block in range(BLOCKS):
-                        project(
-                            chunk * CHUNK + i,
-                            block,
-                            words_of[chunk][:, i, block * WORD_BYTES : (block + 1) * WORD_BYTES],
-                        )
-            ahead = period + 2
-            if ahead < PERIODS - 1:
-                load_scales(ahead)
-                for chunk in range(ahead * PERIOD_CHUNKS, (ahead + 1) * PERIOD_CHUNKS):
-                    words_of[chunk] = load_words(chunk)
-            if ahead == PERIODS - 1:
-                load_scales(ahead)
+        plain_chunks = (PERIODS - 1) * PERIOD_CHUNKS
+        for chunk in range(plain_chunks):
+            for i in range(CHUNK):
+                for block in range(BLOCKS):
+                    project(
+                        chunk * CHUNK + i,
+                        block,
+                        words_of[chunk][:, i, block * WORD_BYTES : (block + 1) * WORD_BYTES],
+                    )
+            ahead = chunk + RING
+            if ahead < plain_chunks:
+                words_of[ahead] = load_words(ahead)
+            if ahead == plain_chunks:
                 for block in last_blocks:
-                    for chunk in range(ahead * PERIOD_CHUNKS, (ahead + 1) * PERIOD_CHUNKS):
-                        g0 = chunk * CHUNK
+                    for late in range(plain_chunks, plain_chunks + PERIOD_CHUNKS):
+                        g0 = late * CHUNK
                         piece = tail.tile([P, CHUNK, WORD_BYTES], U8, name="piece", align_bytes=64)
                         if block < Q_BLOCKS:
                             source = wq_words[g0 : g0 + CHUNK, :, block * (WORD_BYTES // 4) : (block + 1) * (WORD_BYTES // 4)]
                         else:
                             source = wk_words[g0 : g0 + CHUNK]
                         nc.sync.dma_start(out=piece[:].bitcast(I32), in_=source.rearrange("g p b -> p g b"))
-                        last_words[(block, chunk)] = piece
+                        last_words[(block, late)] = piece
 
         for block in last_blocks:
             for chunk in range((PERIODS - 1) * PERIOD_CHUNKS, PERIODS * PERIOD_CHUNKS):

@@ -35,6 +35,7 @@ PERIOD = 8
 PERIODS = GROUPS // PERIOD
 PERIOD_CHUNKS = PERIOD // CHUNK
 RING = 3
+EARLY_PERIODS = 2
 
 X_LOAD = 8
 QUANT = 4
@@ -61,8 +62,7 @@ def tile_qwen3nextattentionforengine_pa_k_kernel(
     x_rows = hidden_states.rearrange("b s k -> (b s) k")
     wq_words = Wq_query_words.bitcast(I32)
     wk_words = Wk_words.bitcast(I32)
-    wq_scales = Wq_query_scales.bitcast(F32)
-    wk_scales = Wk_scales.bitcast(F32)
+    scale_rows = ((Wq_query_scales, 0, Q_BLOCKS * BLOCK), (Wk_scales, K_BLOCK * BLOCK, BLOCK))
     out_q = out_0.rearrange("b s h d -> (b s) (h d)")
     out_k = out_1.rearrange("b s h d -> (b s) (h d)")
 
@@ -88,18 +88,29 @@ def tile_qwen3nextattentionforengine_pa_k_kernel(
         straight_tab = [keep.tile([P, HEAD], F32, name="straight_tab%d" % i) for i in range(2)]
         crossed_tab = [keep.tile([P, HEAD], F32, name="crossed_tab%d" % i) for i in range(2)]
 
-        def load_scales(period):
+        def load_scales_early(period):
             g0 = period * PERIOD
-            plane = planes[period]
-            for rows, first, width in ((wq_scales, 0, Q_BLOCKS * BLOCK), (wk_scales, K_BLOCK * BLOCK, BLOCK)):
+            for rows, first, width in scale_rows:
+                for q in range(8):
+                    low = 32 * (q // 4) + q % 4
+                    nc.sync.dma_start(
+                        out=planes[period][low:P:64, :, first : first + width].bitcast(I32),
+                        in_=rows.bitcast(I32)[g0 : g0 + PERIOD, q:16:8, :].rearrange("g q n -> q g n"),
+                    )
+
+        def load_scales_late(period):
+            g0 = period * PERIOD
+            for rows, first, width in scale_rows:
                 for r in range(4):
                     nc.gpsimd.dma_start(
-                        out=plane[r:P:32, :, first : first + width].bitcast(F32),
-                        in_=rows[g0 : g0 + PERIOD, r:16:4, :].rearrange("g q n -> q g n"),
+                        out=planes[period][r:P:32, :, first : first + width].bitcast(F32),
+                        in_=rows.bitcast(F32)[g0 : g0 + PERIOD, r:16:4, :].rearrange("g q n -> q g n"),
                     )
 
         def load_words(chunk):
             g0 = chunk * CHUNK
+            if chunk % PERIOD_CHUNKS == 0 and chunk // PERIOD_CHUNKS < EARLY_PERIODS:
+                load_scales_early(chunk // PERIOD_CHUNKS)
             words = ring.tile([P, CHUNK, BLOCKS * WORD_BYTES], U8, name="words", align_bytes=64)
             nc.sync.dma_start(
                 out=words[:, :, 0 : Q_BLOCKS * WORD_BYTES].bitcast(I32),
@@ -126,8 +137,8 @@ def tile_qwen3nextattentionforengine_pa_k_kernel(
         for plane in planes:
             nc.vector.memset(plane[:].bitcast(I32), 0)
         masks.make_identity(nc, ident[:])
-        for period in range(PERIODS):
-            load_scales(period)
+        for period in range(EARLY_PERIODS, PERIODS):
+            load_scales_late(period)
         nc.scalar.dma_start(out=cos_sb[:], in_=cos.rearrange("b s d -> (b s) d"))
         nc.scalar.dma_start(out=sin_sb[:], in_=sin.rearrange("b s d -> (b s) d"))
         nc.scalar.dma_start(out=gain[0][:], in_=q_norm_w.partition_broadcast(P))

@@ -34,8 +34,6 @@ CHUNK = 4
 PERIOD = 8
 PERIODS = GROUPS // PERIOD
 PERIOD_CHUNKS = PERIOD // CHUNK
-RING = 3
-EARLY_PERIODS = 2
 
 X_LOAD = 8
 QUANT = 4
@@ -62,21 +60,22 @@ def tile_qwen3nextattentionforengine_pa_k_kernel(
     x_rows = hidden_states.rearrange("b s k -> (b s) k")
     wq_words = Wq_query_words.bitcast(I32)
     wk_words = Wk_words.bitcast(I32)
-    scale_rows = ((Wq_query_scales, 0, Q_BLOCKS * BLOCK), (Wk_scales, K_BLOCK * BLOCK, BLOCK))
+    wq_scales = Wq_query_scales.bitcast(I32)
+    wk_scales = Wk_scales.bitcast(I32)
     out_q = out_0.rearrange("b s h d -> (b s) (h d)")
     out_k = out_1.rearrange("b s h d -> (b s) (h d)")
 
     with ExitStack() as ctx:
         ctx.enter_context(tc.manual_schedule())
         keep = ctx.enter_context(tc.tile_pool(name="keep", bufs=1))
-        ring = ctx.enter_context(tc.tile_pool(name="ring", bufs=RING))
+        ring = ctx.enter_context(tc.tile_pool(name="ring", bufs=2 * PERIOD_CHUNKS))
         sums = ctx.enter_context(tc.psum_pool(name="sums", bufs=1))
 
         x_codes = keep.tile([P, GROUPS, TOKENS], U32, name="x_codes", align_bytes=64)
         x_scales = keep.tile([P, GROUPS, TOKENS], U8, name="x_scales", align_bytes=64)
         planes = [
             keep.tile([P, PERIOD, BLOCKS * BLOCK], U8, name="planes%d" % s, align_bytes=64)
-            for s in range(PERIODS)
+            for s in range(2)
         ]
         acc = [sums.tile([P, BLOCK], F32, name="acc%d" % b) for b in range(BLOCKS)]
         ident = keep.tile([P, P], F32, name="ident")
@@ -84,33 +83,24 @@ def tile_qwen3nextattentionforengine_pa_k_kernel(
         warm = keep.tile([P, 1], F32, name="warm")
         cos_sb = keep.tile([P, HEAD], BF16, name="cos_sb")
         sin_sb = keep.tile([P, HEAD], BF16, name="sin_sb")
-        gain = [keep.tile([P, HEAD], BF16, name="gain%d" % i) for i in range(2)]
+        gain_row = keep.tile([P, 2 * HEAD], BF16, name="gain_row")
+        ones = keep.tile([P, P], BF16, name="ones")
         straight_tab = [keep.tile([P, HEAD], F32, name="straight_tab%d" % i) for i in range(2)]
         crossed_tab = [keep.tile([P, HEAD], F32, name="crossed_tab%d" % i) for i in range(2)]
 
-        def load_scales_early(period):
+        def load_scales(period):
             g0 = period * PERIOD
-            for rows, first, width in scale_rows:
+            plane = planes[period % 2]
+            for rows, first, width in ((wq_scales, 0, Q_BLOCKS * BLOCK), (wk_scales, K_BLOCK * BLOCK, BLOCK)):
                 for q in range(8):
                     low = 32 * (q // 4) + q % 4
                     nc.sync.dma_start(
-                        out=planes[period][low:P:64, :, first : first + width].bitcast(I32),
-                        in_=rows.bitcast(I32)[g0 : g0 + PERIOD, q:16:8, :].rearrange("g q n -> q g n"),
-                    )
-
-        def load_scales_late(period):
-            g0 = period * PERIOD
-            for rows, first, width in scale_rows:
-                for r in range(4):
-                    nc.gpsimd.dma_start(
-                        out=planes[period][r:P:32, :, first : first + width].bitcast(F32),
-                        in_=rows.bitcast(F32)[g0 : g0 + PERIOD, r:16:4, :].rearrange("g q n -> q g n"),
+                        out=plane[low:P:64, :, first : first + width].bitcast(I32),
+                        in_=rows[g0 : g0 + PERIOD, q:16:8, :].rearrange("g q n -> q g n"),
                     )
 
         def load_words(chunk):
             g0 = chunk * CHUNK
-            if chunk % PERIOD_CHUNKS == 0 and chunk // PERIOD_CHUNKS < EARLY_PERIODS:
-                load_scales_early(chunk // PERIOD_CHUNKS)
             words = ring.tile([P, CHUNK, BLOCKS * WORD_BYTES], U8, name="words", align_bytes=64)
             nc.sync.dma_start(
                 out=words[:, :, 0 : Q_BLOCKS * WORD_BYTES].bitcast(I32),
@@ -128,7 +118,7 @@ def tile_qwen3nextattentionforengine_pa_k_kernel(
                 lhsT=x_codes[:, g, :].bitcast(FP8X4),
                 lhsT_scale=x_scales[:, g, :],
                 rhs=words.bitcast(FP4X4),
-                rhs_scale=planes[g // PERIOD][:, g % PERIOD, block * BLOCK : (block + 1) * BLOCK],
+                rhs_scale=planes[(g // PERIOD) % 2][:, g % PERIOD, block * BLOCK : (block + 1) * BLOCK],
                 start=(g == 0),
                 stop=(g == GROUPS - 1),
             )
@@ -137,12 +127,12 @@ def tile_qwen3nextattentionforengine_pa_k_kernel(
         for plane in planes:
             nc.vector.memset(plane[:].bitcast(I32), 0)
         masks.make_identity(nc, ident[:])
-        for period in range(EARLY_PERIODS, PERIODS):
-            load_scales_late(period)
         nc.scalar.dma_start(out=cos_sb[:], in_=cos.rearrange("b s d -> (b s) d"))
         nc.scalar.dma_start(out=sin_sb[:], in_=sin.rearrange("b s d -> (b s) d"))
-        nc.scalar.dma_start(out=gain[0][:], in_=q_norm_w.partition_broadcast(P))
-        nc.scalar.dma_start(out=gain[1][:], in_=k_norm_w.partition_broadcast(P))
+        nc.gpsimd.memset(gain_row[:], 0.0)
+        nc.gpsimd.memset(ones[:], 1.0)
+        nc.scalar.dma_start(out=gain_row[0:1, 0:HEAD], in_=q_norm_w.unsqueeze(0))
+        nc.scalar.dma_start(out=gain_row[0:1, HEAD : 2 * HEAD], in_=k_norm_w.unsqueeze(0))
         nc.scalar.activation(out=warm[:], in_=eps[:], func=ACT.Sqrt)
 
         with ExitStack() as head:
@@ -178,11 +168,16 @@ def tile_qwen3nextattentionforengine_pa_k_kernel(
                 )
 
         words_of = {}
-        for chunk in range(RING):
-            words_of[chunk] = load_words(chunk)
+        for period in range(2):
+            load_scales(period)
+            for chunk in range(period * PERIOD_CHUNKS, (period + 1) * PERIOD_CHUNKS):
+                words_of[chunk] = load_words(chunk)
 
+        spread = acc[0][:, 0 : 2 * HEAD]
+        nc.tensor.matmul(out=spread, lhsT=ones[:], rhs=gain_row[:], start=True, stop=True)
+        gain = [spread[:, i * HEAD : (i + 1) * HEAD] for i in range(2)]
         for i in range(2):
-            nc.vector.tensor_tensor(out=straight_tab[i][:], in0=cos_sb[:], in1=gain[i][:], op=ALU.mult)
+            nc.vector.tensor_tensor(out=straight_tab[i][:], in0=gain[i], in1=cos_sb[:], op=ALU.mult)
             nc.vector.scalar_tensor_tensor(
                 out=crossed_tab[i][:, 0:HALF],
                 in0=sin_sb[:, 0:HALF],
@@ -192,7 +187,7 @@ def tile_qwen3nextattentionforengine_pa_k_kernel(
                 op1=ALU.mult,
             )
             nc.vector.tensor_tensor(
-                out=crossed_tab[i][:, HALF:HEAD], in0=sin_sb[:, HALF:HEAD], in1=gain[i][:, 0:HALF], op=ALU.mult
+                out=crossed_tab[i][:, HALF:HEAD], in0=gain[i][:, 0:HALF], in1=sin_sb[:, HALF:HEAD], op=ALU.mult
             )
 
         tail = ctx.enter_context(tc.tile_pool(name="tail", bufs=BLOCKS * PERIOD_CHUNKS))
@@ -248,29 +243,32 @@ def tile_qwen3nextattentionforengine_pa_k_kernel(
 
         last_blocks = [K_BLOCK] + list(range(Q_BLOCKS))
         last_words = {}
-        plain_chunks = (PERIODS - 1) * PERIOD_CHUNKS
-        for chunk in range(plain_chunks):
-            for i in range(CHUNK):
-                for block in range(BLOCKS):
-                    project(
-                        chunk * CHUNK + i,
-                        block,
-                        words_of[chunk][:, i, block * WORD_BYTES : (block + 1) * WORD_BYTES],
-                    )
-            ahead = chunk + RING
-            if ahead < plain_chunks:
-                words_of[ahead] = load_words(ahead)
-            if ahead == plain_chunks:
+        for period in range(PERIODS - 1):
+            for chunk in range(period * PERIOD_CHUNKS, (period + 1) * PERIOD_CHUNKS):
+                for i in range(CHUNK):
+                    for block in range(BLOCKS):
+                        project(
+                            chunk * CHUNK + i,
+                            block,
+                            words_of[chunk][:, i, block * WORD_BYTES : (block + 1) * WORD_BYTES],
+                        )
+            ahead = period + 2
+            if ahead < PERIODS - 1:
+                load_scales(ahead)
+                for chunk in range(ahead * PERIOD_CHUNKS, (ahead + 1) * PERIOD_CHUNKS):
+                    words_of[chunk] = load_words(chunk)
+            if ahead == PERIODS - 1:
+                load_scales(ahead)
                 for block in last_blocks:
-                    for late in range(plain_chunks, plain_chunks + PERIOD_CHUNKS):
-                        g0 = late * CHUNK
+                    for chunk in range(ahead * PERIOD_CHUNKS, (ahead + 1) * PERIOD_CHUNKS):
+                        g0 = chunk * CHUNK
                         piece = tail.tile([P, CHUNK, WORD_BYTES], U8, name="piece", align_bytes=64)
                         if block < Q_BLOCKS:
                             source = wq_words[g0 : g0 + CHUNK, :, block * (WORD_BYTES // 4) : (block + 1) * (WORD_BYTES // 4)]
                         else:
                             source = wk_words[g0 : g0 + CHUNK]
                         nc.sync.dma_start(out=piece[:].bitcast(I32), in_=source.rearrange("g p b -> p g b"))
-                        last_words[(block, late)] = piece
+                        last_words[(block, chunk)] = piece
 
         for block in last_blocks:
             for chunk in range((PERIODS - 1) * PERIOD_CHUNKS, PERIODS * PERIOD_CHUNKS):

@@ -29,6 +29,7 @@ Q_BLOCKS = 4
 K_BLOCK = 4
 BLOCKS = 5
 WORD_BYTES = BLOCK * 2
+GAP = 64
 
 CHUNK = 4
 PERIOD = 8
@@ -262,12 +263,13 @@ def tile_qwen3nextattentionforengine_pa_k_kernel(
                 for block in last_blocks:
                     for chunk in range(ahead * PERIOD_CHUNKS, (ahead + 1) * PERIOD_CHUNKS):
                         g0 = chunk * CHUNK
-                        piece = tail.tile([P, CHUNK, WORD_BYTES], U8, name="piece", align_bytes=64)
+                        padded = tail.tile([P, CHUNK, WORD_BYTES + GAP], U8, name="padded", align_bytes=64)
+                        piece = padded[:, :, 0:WORD_BYTES]
                         if block < Q_BLOCKS:
                             source = wq_words[g0 : g0 + CHUNK, :, block * (WORD_BYTES // 4) : (block + 1) * (WORD_BYTES // 4)]
                         else:
                             source = wk_words[g0 : g0 + CHUNK]
-                        nc.sync.dma_start(out=piece[:].bitcast(I32), in_=source.rearrange("g p b -> p g b"))
+                        nc.sync.dma_start(out=piece.bitcast(I32), in_=source.rearrange("g p b -> p g b"))
                         last_words[(block, chunk)] = piece
 
         for block in last_blocks:

from contextlib import ExitStack

import concourse.masks as masks
import concourse.mybir as mybir

F32 = mybir.dt.float32
BF16 = mybir.dt.bfloat16
I32 = mybir.dt.int32
U32 = mybir.dt.uint32
U8 = mybir.dt.uint8
FP8X4 = mybir.dt.float8_e4m3fn_x4
FP4X4 = mybir.dt.float4_e2m1fn_x4
ACT = mybir.ActivationFunctionType
ALU = mybir.AluOpType

P = 128
TOKENS = 128
HIDDEN = 16384
PACK = 4
K_PASS = P * PACK
GROUPS = HIDDEN // K_PASS
HEAD = 128
HALF = HEAD // 2
EPS = 1e-6

BLOCK = 512
BLOCK_HEADS = BLOCK // HEAD
Q_BLOCKS = 4
K_BLOCK = 4
BLOCKS = 5
WORD_BYTES = BLOCK * 2
GAP = 64

CHUNK = 4
PERIOD = 8
PERIODS = GROUPS // PERIOD
PERIOD_CHUNKS = PERIOD // CHUNK

X_LOAD = 8
QUANT = 4
BANK = 2

FLOPS = 2 * TOKENS * HIDDEN * BLOCKS * BLOCK


def tile_qwen3nextattentionforengine_pa_k_kernel(
    tc,
    hidden_states,
    cos,
    sin,
    Wq_query_words,
    Wq_query_scales,
    Wk_words,
    Wk_scales,
    q_norm_w,
    k_norm_w,
    out_0,
    out_1,
):
    nc = tc.nc
    x_rows = hidden_states.rearrange("b s k -> (b s) k")
    wq_words = Wq_query_words.bitcast(I32)
    wk_words = Wk_words.bitcast(I32)
    wq_scales = Wq_query_scales.bitcast(I32)
    wk_scales = Wk_scales.bitcast(I32)
    out_q = out_0.rearrange("b s h d -> (b s) (h d)")
    out_k = out_1.rearrange("b s h d -> (b s) (h d)")

    with ExitStack() as ctx:
        ctx.enter_context(tc.manual_schedule())
        keep = ctx.enter_context(tc.tile_pool(name="keep", bufs=1))
        ring = ctx.enter_context(tc.tile_pool(name="ring", bufs=2 * PERIOD_CHUNKS))
        sums = ctx.enter_context(tc.psum_pool(name="sums", bufs=1))

        x_codes = keep.tile([P, GROUPS, TOKENS], U32, name="x_codes", align_bytes=64)
        x_scales = keep.tile([P, GROUPS, TOKENS], U8, name="x_scales", align_bytes=64)
        planes = [
            keep.tile([P, PERIOD, BLOCKS * BLOCK], U8, name="planes%d" % s, align_bytes=64)
            for s in range(2)
        ]
        acc = [sums.tile([P, BLOCK], F32, name="acc%d" % b) for b in range(BLOCKS)]
        ident = keep.tile([P, P], F32, name="ident")
        eps = keep.tile([P, 1], F32, name="eps")
        warm = keep.tile([P, 1], F32, name="warm")
        cos_sb = keep.tile([P, HEAD], BF16, name="cos_sb")
        sin_sb = keep.tile([P, HEAD], BF16, name="sin_sb")
        gain_row = keep.tile([P, 2 * HEAD], BF16, name="gain_row")
        ones = keep.tile([P, P], BF16, name="ones")
        straight_tab = [keep.tile([P, HEAD], F32, name="straight_tab%d" % i) for i in range(2)]
        crossed_tab = [keep.tile([P, HEAD], F32, name="crossed_tab%d" % i) for i in range(2)]

        def load_scales(period):
            g0 = period * PERIOD
            plane = planes[period % 2]
            for rows, first, width in ((wq_scales, 0, Q_BLOCKS * BLOCK), (wk_scales, K_BLOCK * BLOCK, BLOCK)):
                for q in range(8):
                    low = 32 * (q // 4) + q % 4
                    nc.sync.dma_start(
                        out=plane[low:P:64, :, first : first + width].bitcast(I32),
                        in_=rows[g0 : g0 + PERIOD, q:16:8, :].rearrange("g q n -> q g n"),
                    )

        def load_words(chunk):
            g0 = chunk * CHUNK
            words = ring.tile([P, CHUNK, BLOCKS * WORD_BYTES], U8, name="words", align_bytes=64)
            nc.sync.dma_start(
                out=words[:, :, 0 : Q_BLOCKS * WORD_BYTES].bitcast(I32),
                in_=wq_words[g0 : g0 + CHUNK].rearrange("g p b -> p g b"),
            )
            nc.sync.dma_start(
                out=words[:, :, K_BLOCK * WORD_BYTES :].bitcast(I32),
                in_=wk_words[g0 : g0 + CHUNK].rearrange("g p b -> p g b"),
            )
            return words

        def project(g, block, words):
            nc.tensor.matmul_mx(
                out=acc[block][:],
                lhsT=x_codes[:, g, :].bitcast(FP8X4),
                lhsT_scale=x_scales[:, g, :],
                rhs=words.bitcast(FP4X4),
                rhs_scale=planes[(g // PERIOD) % 2][:, g % PERIOD, block * BLOCK : (block + 1) * BLOCK],
                start=(g == 0),
                stop=(g == GROUPS - 1),
            )

        nc.vector.memset(eps[:], EPS)
        for plane in planes:
            nc.vector.memset(plane[:].bitcast(I32), 0)
        masks.make_identity(nc, ident[:])
        nc.scalar.dma_start(out=cos_sb[:], in_=cos.rearrange("b s d -> (b s) d"))
        nc.scalar.dma_start(out=sin_sb[:], in_=sin.rearrange("b s d -> (b s) d"))
        nc.gpsimd.memset(gain_row[:], 0.0)
        nc.gpsimd.memset(ones[:], 1.0)
        nc.scalar.dma_start(out=gain_row[0:1, 0:HEAD], in_=q_norm_w.unsqueeze(0))
        nc.scalar.dma_start(out=gain_row[0:1, HEAD : 2 * HEAD], in_=k_norm_w.unsqueeze(0))
        nc.scalar.activation(out=warm[:], in_=eps[:], func=ACT.Sqrt)

        with ExitStack() as head:
            x_pool = head.enter_context(tc.tile_pool(name="x_pool", bufs=GROUPS // X_LOAD))
            stage = head.enter_context(tc.tile_pool(name="stage", bufs=2))
            flipped = head.enter_context(tc.psum_pool(name="flipped", bufs=3))

            x_raw = []
            for c in range(GROUPS // X_LOAD):
                raw = x_pool.tile([P, X_LOAD * K_PASS], BF16, name="raw")
                nc.sync.dma_start(out=raw[:], in_=x_rows[:, c * X_LOAD * K_PASS : (c + 1) * X_LOAD * K_PASS])
                x_raw.append(raw)

            for g0 in range(0, GROUPS, QUANT):
                pairs = x_raw[g0 // X_LOAD][:].bitcast(F32)
                grouped = stage.tile([P, QUANT, TOKENS, PACK], BF16, name="grouped", align_bytes=64)
                for b0 in range(0, QUANT, BANK):
                    xt = flipped.tile([P, BANK, 2, TOKENS], F32, name="xt")
                    for i in range(BANK):
                        first = ((g0 + b0 + i) % X_LOAD) * (K_PASS // 2)
                        for u in range(2):
                            nc.tensor.transpose(
                                xt[:, i, u, :], pairs[:, first + u : first + K_PASS // 2 : 2], ident[:]
                            )
                    nc.scalar.copy(
                        out=grouped[:, b0 : b0 + BANK, :, :].bitcast(F32),
                        in_=xt[:].rearrange("p g u m -> p g m u"),
                    )
                nc.vector.quantize_mx(
                    out=x_codes[:, g0 : g0 + QUANT, :].rearrange("p g m -> p (g m)").bitcast(FP8X4),
                    scales=x_scales[:, g0 : g0 + QUANT, :].rearrange("p g m -> p (g m)"),
                    in_=grouped[:].rearrange("p g m t -> p (g m t)"),
                )

        words_of = {}
        for period in range(2):
            load_scales(period)
            for chunk in range(period * PERIOD_CHUNKS, (period + 1) * PERIOD_CHUNKS):
                words_of[chunk] = load_words(chunk)

        spread = acc[0][:, 0 : 2 * HEAD]
        nc.tensor.matmul(out=spread, lhsT=ones[:], rhs=gain_row[:], start=True, stop=True)
        gain = [spread[:, i * HEAD : (i + 1) * HEAD] for i in range(2)]
        for i in range(2):
            nc.vector.tensor_tensor(out=straight_tab[i][:], in0=gain[i], in1=cos_sb[:], op=ALU.mult)
            nc.vector.scalar_tensor_tensor(
                out=crossed_tab[i][:, 0:HALF],
                in0=sin_sb[:, 0:HALF],
                scalar=-1.0,
                in1=gain[i][:, HALF:HEAD],
                op0=ALU.mult,
                op1=ALU.mult,
            )
            nc.vector.tensor_tensor(
                out=crossed_tab[i][:, HALF:HEAD], in0=gain[i][:, 0:HALF], in1=sin_sb[:, HALF:HEAD], op=ALU.mult
            )

        tail = ctx.enter_context(tc.tile_pool(name="tail", bufs=BLOCKS * PERIOD_CHUNKS))
        work = ctx.enter_context(tc.tile_pool(name="work", bufs=2))

        def finish(block):
            i = 0 if block < Q_BLOCKS else 1
            dest = out_q[:, block * BLOCK : (block + 1) * BLOCK] if block < Q_BLOCKS else out_k
            heads = acc[block][:].rearrange("p (h d) -> p h d", d=HEAD)
            v = work.tile([P, BLOCK_HEADS, HEAD], F32, name="v")
            squares = work.tile([P, BLOCK_HEADS, HEAD], F32, name="squares")
            sum_sq = work.tile([P, BLOCK_HEADS], F32, name="sum_sq")
            rms = work.tile([P, BLOCK_HEADS], F32, name="rms")
            inv_rms = work.tile([P, BLOCK_HEADS], F32, name="inv_rms")
            straight = work.tile([P, BLOCK_HEADS, HEAD], F32, name="straight")
            crossed = work.tile([P, BLOCK_HEADS, HEAD], F32, name="crossed")
            result = work.tile([P, BLOCK_HEADS, HEAD], F32, name="result")

            nc.scalar.copy(out=v[:], in_=heads)
            for h in range(BLOCK_HEADS):
                nc.scalar.activation(
                    out=squares[:, h, :], in_=heads[:, h, :], func=ACT.Square, accum_out=sum_sq[:, h : h + 1]
                )
            nc.scalar.activation(out=rms[:], in_=sum_sq[:], func=ACT.Sqrt, scale=1.0 / HEAD, bias=eps[:])

            nc.vector.tensor_tensor(
                out=straight[:],
                in0=v[:],
                in1=straight_tab[i][:].unsqueeze(1).to_broadcast([P, BLOCK_HEADS, HEAD]),
                op=ALU.mult,
            )
            nc.vector.tensor_tensor(
                out=crossed[:, :, 0:HALF],
                in0=v[:, :, HALF:HEAD],
                in1=crossed_tab[i][:, 0:HALF].unsqueeze(1).to_broadcast([P, BLOCK_HEADS, HALF]),
                op=ALU.mult,
            )
            nc.vector.tensor_tensor(
                out=crossed[:, :, HALF:HEAD],
                in0=v[:, :, 0:HALF],
                in1=crossed_tab[i][:, HALF:HEAD].unsqueeze(1).to_broadcast([P, BLOCK_HEADS, HALF]),
                op=ALU.mult,
            )
            nc.vector.tensor_tensor(out=straight[:], in0=straight[:], in1=crossed[:], op=ALU.add)
            nc.vector.reciprocal(out=inv_rms[:], in_=rms[:])
            nc.vector.tensor_tensor(
                out=result[:],
                in0=straight[:],
                in1=inv_rms[:].unsqueeze(2).to_broadcast([P, BLOCK_HEADS, HEAD]),
                op=ALU.mult,
            )
            nc.sync.dma_start(out=dest, in_=result[:].rearrange("p h d -> p (h d)"))

        last_blocks = [K_BLOCK] + list(range(Q_BLOCKS))
        last_words = {}
        for period in range(PERIODS - 1):
            for chunk in range(period * PERIOD_CHUNKS, (period + 1) * PERIOD_CHUNKS):
                for i in range(CHUNK):
                    for block in range(BLOCKS):
                        project(
                            chunk * CHUNK + i,
                            block,
                            words_of[chunk][:, i, block * WORD_BYTES : (block + 1) * WORD_BYTES],
                        )
            ahead = period + 2
            if ahead < PERIODS - 1:
                load_scales(ahead)
                for chunk in range(ahead * PERIOD_CHUNKS, (ahead + 1) * PERIOD_CHUNKS):
                    words_of[chunk] = load_words(chunk)
            if ahead == PERIODS - 1:
                load_scales(ahead)
                for block in last_blocks:
                    for chunk in range(ahead * PERIOD_CHUNKS, (ahead + 1) * PERIOD_CHUNKS):
                        g0 = chunk * CHUNK
                        padded = tail.tile([P, CHUNK, WORD_BYTES + GAP], U8, name="padded", align_bytes=64)
                        piece = padded[:, :, 0:WORD_BYTES]
                        if block < Q_BLOCKS:
                            source = wq_words[g0 : g0 + CHUNK, :, block * (WORD_BYTES // 4) : (block + 1) * (WORD_BYTES // 4)]
                        else:
                            source = wk_words[g0 : g0 + CHUNK]
                        nc.sync.dma_start(out=piece.bitcast(I32), in_=source.rearrange("g p b -> p g b"))
                        last_words[(block, chunk)] = piece

        for block in last_blocks:
            for chunk in range((PERIODS - 1) * PERIOD_CHUNKS, PERIODS * PERIOD_CHUNKS):
                for i in range(CHUNK):
                    project(chunk * CHUNK + i, block, last_words[(block, chunk)][:, i, :])
            finish(block)
